import numpy as np
import ml_dtypes


def mxq(x, axis, fmt="e4m3"):
    dtype, down = {"e4m3": (ml_dtypes.float8_e4m3fn, 7), "e5m2": (ml_dtypes.float8_e5m2, 14)}[fmt]
    v = np.moveaxis(np.asarray(x, np.float32).astype(ml_dtypes.bfloat16).astype(np.float64), axis, -1)
    blocks = v.reshape(v.shape[:-1] + (-1, 32))
    amax = np.abs(blocks).max(-1, keepdims=True)
    byte = np.maximum(np.where(amax > 0, np.frexp(amax)[1] - 1 + 127, 0) - down, 1)
    scale = np.exp2(byte - 127.0)
    codes = (blocks / scale).astype(np.float32).astype(dtype).astype(np.float64)
    return np.moveaxis((codes * scale).reshape(v.shape), -1, axis)


WIDE = False


def mx_kscale(k):
    if not WIDE:
        return np.ones(k)
    levels = np.array([30, -30])
    if k % 512:
        return np.exp2(np.random.permutation(np.resize(levels, k // 32))).repeat(32)
    a = np.empty((k // 512, 16))
    for p in range(k // 512):
        a[p, :8] = np.random.permutation(np.resize(levels, 8))
        for g in range(8):
            far = levels[np.abs(levels - a[p, g]) >= 10]
            a[p, g + 8] = far[np.random.randint(len(far))]
    return np.exp2(a.ravel()).repeat(32)


BF16 = ml_dtypes.bfloat16


def bf(x):
    return np.asarray(x, np.float32).astype(BF16)


def f64(x):
    return np.asarray(x).astype(np.float64)


E2M1 = np.array([0.0, 0.5, 1.0, 1.5, 2.0, 3.0, 4.0, 6.0, -0.0, -0.5, -1.0, -1.5, -2.0, -3.0, -4.0, -6.0])


def pack_weight(w, fmt):
    k, n = w.shape
    w = f64(bf(w)).reshape(k // 32, 32, n)
    amax = np.abs(w).max(1)
    if fmt == "e4m3":
        byte = np.frexp(amax)[1] - 1 + 127 - 7
    else:
        mant, ex = np.frexp(amax / 6.0)
        byte = np.where(mant > 0.5, ex, ex - 1) + 127
    byte = np.clip(np.where(amax > 0, byte, 1), 1, 254)
    scaled = (w * np.exp2(127.0 - byte)[:, None, :]).reshape(k, n).astype(np.float32)
    by_word = np.ascontiguousarray(scaled.reshape(k // 512, 128, 4, n).transpose(0, 1, 3, 2))
    if fmt == "e4m3":
        words = by_word.astype(ml_dtypes.float8_e4m3fn).view(np.uint8)
    else:
        c = by_word.astype(ml_dtypes.float4_e2m1fn).view(np.uint8) & 0xF
        words = c[..., 0::2] | (c[..., 1::2] << 4)
    return np.ascontiguousarray(words), np.ascontiguousarray(byte.astype(np.uint8).reshape(k // 512, 16, n))


def unpack_weight(words, scales, fmt):
    g, p, n, _ = words.shape
    if fmt == "e4m3":
        vals = np.ascontiguousarray(words).view(ml_dtypes.float8_e4m3fn).astype(np.float64)
    else:
        nib = np.empty((g, p, n, 4), np.uint8)
        nib[..., 0::2] = words & 0xF
        nib[..., 1::2] = words >> 4
        vals = E2M1[nib]
    vals = vals * np.repeat(np.exp2(scales.astype(np.float64) - 127.0), 8, axis=1)[..., None]
    return vals.transpose(0, 1, 3, 2).reshape(g * 512, n)

def pack4(w):
    words, scales = pack_weight(w, "e2m1")
    return words.reshape(words.shape[0], 128, -1), scales


def unpack4(words, scales):
    return unpack_weight(words.reshape(words.shape[0], 128, -1, 2), scales, "e2m1")


B, T, C, H, W = 1, 1536, 1024, 8, 512
D = C // H
HALF = D // 2
ROPE_BASE = 10000.0


def rotate_half(u):
    return np.concatenate([-u[..., HALF:], u[..., :HALF]], axis=-1)


def setup_inputs():
    s = mx_kscale(C)
    start = np.random.randint(0, T)
    inv_freq = 1.0 / (ROPE_BASE ** (np.arange(0, D, 2) / D))
    freqs = np.outer(start + np.arange(T), inv_freq)
    emb = np.concatenate([freqs, freqs], axis=-1)
    x = bf(np.random.standard_normal((B, T, C)) * s)
    words, scales = pack4(np.random.standard_normal((C, 3 * C)) * 1.25 / np.sqrt(C) / s[:, None])
    return {"x": x,
            "freqs_cos": bf(np.cos(emb)),
            "freqs_sin": bf(np.sin(emb)),
            "w_attn_words": words,
            "w_attn_scales": scales}


def reference(x, freqs_cos, freqs_sin, w_attn_words, w_attn_scales):
    qkv = mxq(f64(x), 2, "e5m2") @ unpack4(w_attn_words, w_attn_scales)
    q, k, v = np.split(qkv, 3, axis=-1)
    q = q.reshape(B, T, H, D).transpose(0, 2, 1, 3)
    k = k.reshape(B, T, H, D).transpose(0, 2, 1, 3)
    v = v.reshape(B, T, H, D).transpose(0, 2, 1, 3)
    cos = f64(freqs_cos)[None, None, :, :]
    sin = f64(freqs_sin)[None, None, :, :]
    q_rot = q * cos + rotate_half(q) * sin
    k_rot = k * cos + rotate_half(k) * sin
    return q_rot, k_rot, v

@@ -1,0 +1,235 @@
+from contextlib import ExitStack
+
+import concourse.mybir as mybir
+from concourse.masks import make_identity
+
+T, C, H, D = 1536, 1024, 8, 128
+HALF = D // 2
+FLOPS = 2 * T * C * 3 * C
+
+F32 = mybir.dt.float32
+BF16 = mybir.dt.bfloat16
+I32 = mybir.dt.int32
+U32 = mybir.dt.uint32
+U8 = mybir.dt.uint8
+E5M2X4 = mybir.dt.float8_e5m2_x4
+E2M1X4 = mybir.dt.float4_e2m1fn_x4
+ALU = mybir.AluOpType
+ACT = mybir.ActivationFunctionType
+
+P = 128
+TILES = T // P
+PASSES = C // 512
+NCOL = 512
+HEADS = NCOL // D
+PAIR = 2
+
+X_GROUPS = [(0, 1), (1, 1), (2, 2), (4, 4), (8, 4)]
+TABLE_GROUPS = [(0, 2), (2, 10)]
+W_GROUPS = [(0, 1), (1, 1), (2, 2), (4, 2)]
+PLANE_GROUPS = [(0, 2), (2, 4)]
+TRANSPOSE_AFTER = {3: 2, 9: 3, 13: 4}
+QUANTIZE_AFTER = {5: 2, 11: 3, 15: 4}
+V_FIRST, V_LAST = 10, 44
+
+
+def group_of(groups, i):
+    for n, (first, count) in enumerate(groups):
+        if first <= i < first + count:
+            return n, i - first
+    raise ValueError(i)
+
+
+def tile_swaattention_pa_kernel(tc, x, freqs_cos, freqs_sin, w_attn_words, w_attn_scales, out_0, out_1, out_2):
+    nc = tc.nc
+    x_rows = x[0].rearrange("(p j) c -> p (j c)", j=TILES)
+    cos_rows = freqs_cos.rearrange("(p j) d -> p (j d)", j=TILES)
+    sin_rows = freqs_sin.rearrange("(p j) d -> p (j d)", j=TILES)
+    w_rows = w_attn_words.rearrange("g p n -> p g n")
+    outs = [o[0].rearrange("h (p j) d -> p h (j d)", j=TILES) for o in (out_0, out_1, out_2)]
+
+    with ExitStack() as ctx:
+        keep = ctx.enter_context(tc.tile_pool(name="keep", bufs=1))
+        prod = ctx.enter_context(tc.tile_pool(name="prod", bufs=4))
+        res = ctx.enter_context(tc.tile_pool(name="res", bufs=8))
+        rot_ps = ctx.enter_context(tc.psum_pool(name="rot_ps", bufs=4))
+        aux_ps = ctx.enter_context(tc.psum_pool(name="aux_ps", bufs=4))
+        ctx.enter_context(tc.manual_schedule())
+
+        ident = keep.tile([P, P], F32, name="ident")
+        make_identity(nc, ident[:])
+
+        x_sb = [keep.tile([P, n * C], BF16, name="x%d" % f, align_bytes=64) for f, n in X_GROUPS]
+        grouped = [keep.tile([P, n * C], BF16, name="grouped%d" % f, align_bytes=64) for f, n in X_GROUPS]
+        codes = [keep.tile([P, n * C // 4], U32, name="codes%d" % f, align_bytes=64) for f, n in X_GROUPS]
+        scales = [keep.tile([P, n * C // 4], U8, name="scales%d" % f, align_bytes=64) for f, n in X_GROUPS]
+        tables = [keep.tile([P, 5 * n, HALF], BF16, name="tables%d" % f, align_bytes=64) for f, n in TABLE_GROUPS]
+        w_sb = [keep.tile([P, PASSES, n * 2 * NCOL], U8, name="w%d" % f, align_bytes=64) for f, n in W_GROUPS]
+        planes = [keep.tile([P, PASSES, n * NCOL], U8, name="plane%d" % f, align_bytes=64) for f, n in PLANE_GROUPS]
+
+        for plane in planes:
+            nc.vector.memset(plane[:].bitcast(I32), 0)
+
+        def load_x(n):
+            first, count = X_GROUPS[n]
+            nc.sync.dma_start(out=x_sb[n][:], in_=x_rows[:, first * C : (first + count) * C])
+
+        def load_w(n):
+            first, count = W_GROUPS[n]
+            cols = slice(first * 2 * NCOL, (first + count) * 2 * NCOL)
+            nc.sync.dma_start(out=w_sb[n][:].bitcast(I32), in_=w_rows[:, :, cols].bitcast(I32))
+
+        def load_plane(n):
+            first, count = PLANE_GROUPS[n]
+            cols = slice(first * NCOL, (first + count) * NCOL)
+            for q in range(4):
+                nc.sync.dma_start(
+                    out=planes[n][32 * q : 32 * q + 4, :, :].bitcast(I32),
+                    in_=w_attn_scales[:, 4 * q : 4 * q + 4, cols].rearrange("g r n -> r g n").bitcast(I32),
+                )
+
+        def load_tables(n):
+            first, count = TABLE_GROUPS[n]
+            cols = slice(first * D, (first + count) * D)
+            flat = tables[n][:].rearrange("p b d -> p (b d)")
+            nc.sync.dma_start(out=flat[:, count * HALF : 3 * count * HALF], in_=cos_rows[:, cols])
+            nc.sync.dma_start(out=flat[:, 3 * count * HALF : 5 * count * HALF], in_=sin_rows[:, cols])
+
+        load_x(0)
+        load_x(1)
+        load_w(0)
+        load_plane(0)
+        load_tables(0)
+        load_w(1)
+        load_x(2)
+        load_plane(1)
+        load_w(2)
+        load_tables(1)
+        load_x(3)
+        load_w(3)
+        load_x(4)
+
+        def transpose_group(n):
+            banks = []
+            for jj in range(X_GROUPS[n][1]):
+                words = x_sb[n][:, jj * C : (jj + 1) * C].bitcast(F32)
+                bank = aux_ps.tile([P, NCOL], F32, name="aux")
+                for g in range(PASSES):
+                    for u in range(2):
+                        col = (2 * g + u) * P
+                        nc.tensor.transpose(bank[:, col : col + P], words[:, 256 * g + u : 256 * (g + 1) : 2], ident[:])
+                banks.append(bank)
+            return banks
+
+        def interleave(copy, n, banks):
+            for jj, bank in enumerate(banks):
+                dst = grouped[n][:, jj * C : (jj + 1) * C].bitcast(F32)
+                copy(
+                    out=dst.rearrange("p (g r u) -> p g r u", g=PASSES, u=2),
+                    in_=bank[:].rearrange("p (g u r) -> p g r u", g=PASSES, u=2),
+                )
+
+        def quantize(n):
+            nc.vector.quantize_mx(out=codes[n][:].bitcast(E5M2X4), scales=scales[n][:], in_=grouped[n][:])
+
+        def project(bank, j, c):
+            xn, jj = group_of(X_GROUPS, j)
+            wn, wc = group_of(W_GROUPS, c)
+            pn, pc = group_of(PLANE_GROUPS, c)
+            for g in range(PASSES):
+                col = (jj * PASSES + g) * P
+                nc.tensor.matmul_mx(
+                    out=bank[:],
+                    lhsT=codes[xn][:, col : col + P].bitcast(E5M2X4),
+                    lhsT_scale=scales[xn][:, col : col + P],
+                    rhs=w_sb[wn][:, g, wc * 2 * NCOL : (wc + 1) * 2 * NCOL].bitcast(E2M1X4),
+                    rhs_scale=planes[pn][:, g, pc * NCOL : (pc + 1) * NCOL],
+                    start=(g == 0),
+                    stop=(g == PASSES - 1),
+                )
+
+        def products(bank, j, lo_prod, hi_prod):
+            tn, tj = group_of(TABLE_GROUPS, j)
+            count = TABLE_GROUPS[tn][1]
+            neg_sin_lo, cos_lo, sin_lo = tj, count + 2 * tj, 3 * count + 2 * tj
+            with_lo = tables[tn][:, cos_lo : sin_lo + 2 : sin_lo + 1 - cos_lo, :]
+            with_hi = tables[tn][:, neg_sin_lo : cos_lo + 2 : cos_lo + 1 - neg_sin_lo, :]
+            halves = bank[:].rearrange("p (h s d) -> p h s d", s=2, d=HALF)
+            shape = [P, HEADS, 2, HALF]
+            for s, table, dst in ((0, with_lo, lo_prod), (1, with_hi, hi_prod)):
+                nc.vector.tensor_tensor(
+                    out=dst[:, :, j % PAIR, :].rearrange("p h (s d) -> p h s d", s=2),
+                    in0=halves[:, :, s : s + 1, :].to_broadcast(shape),
+                    in1=table.unsqueeze(1).to_broadcast(shape),
+                    op=ALU.mult,
+                )
+
+        def out_view(c, j, count):
+            h0 = (c % 2) * HEADS
+            return outs[c // 2][:, h0 : h0 + HEADS, j * D : (j + count) * D]
+
+        def flat(t):
+            return t[:].rearrange("p h j d -> p (h j d)")
+
+        banks0 = transpose_group(0)
+        banks1 = transpose_group(1)
+        interleave(nc.vector.tensor_copy, 0, banks0)
+        quantize(0)
+        count = TABLE_GROUPS[0][1]
+        nc.vector.tensor_scalar(
+            out=tables[0][:, 0:count, :], in0=tables[0][:, 3 * count : 5 * count : 2, :],
+            scalar1=-1.0, scalar2=None, op0=ALU.mult,
+        )
+        interleave(nc.vector.tensor_copy, 1, banks1)
+        quantize(1)
+
+        rot_steps = [(j0 + jj, c) for j0 in range(0, TILES, PAIR) for c in range(4) for jj in range(PAIR)]
+        v_steps = [(j0 + jj, c) for j0 in range(0, TILES, PAIR) for c in (4, 5) for jj in range(PAIR)]
+        v_done = 0
+        v_res = None
+        lo_prod = hi_prod = None
+        for s, (j, c) in enumerate(rot_steps):
+            bank = rot_ps.tile([P, NCOL], F32, name="rot")
+            project(bank, j, c)
+            if j % PAIR == 0:
+                lo_prod = prod.tile([P, HEADS, PAIR, D], F32, name="lo_prod")
+                hi_prod = prod.tile([P, HEADS, PAIR, D], F32, name="hi_prod")
+            products(bank, j, lo_prod, hi_prod)
+            if j % PAIR == PAIR - 1:
+                j0 = j - (PAIR - 1)
+                rotated = res.tile([P, HEADS, PAIR, D], F32, name="rotated")
+                if s < len(rot_steps) - 1:
+                    nc.gpsimd.tensor_tensor(out=flat(rotated), in0=flat(lo_prod), in1=flat(hi_prod), op=ALU.add)
+                    nc.sync.dma_start(out=out_view(c, j0, PAIR), in_=rotated[:].rearrange("p h j d -> p h (j d)"))
+                else:
+                    for jj in range(PAIR):
+                        nc.vector.tensor_tensor(
+                            out=rotated[:, :, jj, :], in0=lo_prod[:, :, jj, :], in1=hi_prod[:, :, jj, :], op=ALU.add
+                        )
+                        nc.sync.dma_start(out=out_view(c, j0 + jj, 1), in_=rotated[:, :, jj, :])
+
+            if s in QUANTIZE_AFTER:
+                quantize(QUANTIZE_AFTER[s])
+            if s in TRANSPOSE_AFTER:
+                n = TRANSPOSE_AFTER[s]
+                interleave(nc.scalar.copy, n, transpose_group(n))
+                if n == 2:
+                    count = TABLE_GROUPS[1][1]
+                    nc.scalar.activation(
+                        out=tables[1][:, 0:count, :], in_=tables[1][:, 3 * count : 5 * count : 2, :],
+                        func=ACT.Copy, scale=-1.0,
+                    )
+
+            v_due = 0 if s < V_FIRST else min(len(v_steps), (s - V_FIRST + 1) * len(v_steps) // (V_LAST - V_FIRST + 1))
+            while v_done < v_due:
+                vj, vc = v_steps[v_done]
+                v_done += 1
+                v_bank = aux_ps.tile([P, NCOL], F32, name="aux")
+                project(v_bank, vj, vc)
+                if vj % PAIR == 0:
+                    v_res = res.tile([P, HEADS, PAIR, D], F32, name="v_res")
+                nc.scalar.copy(out=v_res[:, :, vj % PAIR, :], in_=v_bank[:].rearrange("p (h d) -> p h d", d=D))
+                if vj % PAIR == PAIR - 1:
+                    nc.scalar.dma_start(
+                        out=out_view(vc, vj - (PAIR - 1), PAIR), in_=v_res[:].rearrange("p h j d -> p h (j d)")
+                    )

@@ -22,15 +22,17 @@ TILES = T // P
 PASSES = C // 512
 NCOL = 512
 HEADS = NCOL // D
-PAIR = 2
 
-X_GROUPS = [(0, 1), (1, 1), (2, 2), (4, 4), (8, 4)]
+X_GROUPS = [(0, 1), (1, 1), (2, 2), (4, 2), (6, 4), (10, 2)]
+OUT_GROUPS = [(0, 2), (2, 4), (6, 4), (10, 2)]
 TABLE_GROUPS = [(0, 2), (2, 10)]
 W_GROUPS = [(0, 1), (1, 1), (2, 2), (4, 2)]
 PLANE_GROUPS = [(0, 2), (2, 4)]
-TRANSPOSE_AFTER = {3: 2, 9: 3, 13: 4}
-QUANTIZE_AFTER = {5: 2, 11: 3, 15: 4}
-V_FIRST, V_LAST = 10, 44
+TRANSPOSE_AFTER = {3: 2, 7: 3, 10: 4, 13: 5}
+QUANTIZE_AFTER = {5: 2, 7: 3, 11: 4, 15: 5}
+V_FIRST, V_LAST = 11, 42
+ADD_SPAN = 2
+VECTOR_ADDS = 6
 
 
 def group_of(groups, i):
@@ -50,8 +52,9 @@ def tile_swaattention_pa_kernel(tc, x, freqs_cos, freqs_sin, w_attn_words, w_att
 
     with ExitStack() as ctx:
         keep = ctx.enter_context(tc.tile_pool(name="keep", bufs=1))
-        prod = ctx.enter_context(tc.tile_pool(name="prod", bufs=4))
-        res = ctx.enter_context(tc.tile_pool(name="res", bufs=8))
+        prod = ctx.enter_context(tc.tile_pool(name="prod", bufs=6))
+        res = ctx.enter_context(tc.tile_pool(name="res", bufs=5))
+        v_pool = ctx.enter_context(tc.tile_pool(name="v_pool", bufs=4))
         rot_ps = ctx.enter_context(tc.psum_pool(name="rot_ps", bufs=4))
         aux_ps = ctx.enter_context(tc.psum_pool(name="aux_ps", bufs=4))
         ctx.enter_context(tc.manual_schedule())
@@ -104,10 +107,11 @@ def tile_swaattention_pa_kernel(tc, x, freqs_cos, freqs_sin, w_attn_words, w_att
         load_x(2)
         load_plane(1)
         load_w(2)
-        load_tables(1)
         load_x(3)
-        load_w(3)
+        load_tables(1)
         load_x(4)
+        load_w(3)
+        load_x(5)
 
         def transpose_group(n):
             banks = []
@@ -148,7 +152,7 @@ def tile_swaattention_pa_kernel(tc, x, freqs_cos, freqs_sin, w_attn_words, w_att
                     stop=(g == PASSES - 1),
                 )
 
-        def products(bank, j, lo_prod, hi_prod):
+        def products(bank, j, jj, lo_prod, hi_prod):
             tn, tj = group_of(TABLE_GROUPS, j)
             count = TABLE_GROUPS[tn][1]
             neg_sin_lo, cos_lo, sin_lo = tj, count + 2 * tj, 3 * count + 2 * tj
@@ -158,7 +162,7 @@ def tile_swaattention_pa_kernel(tc, x, freqs_cos, freqs_sin, w_attn_words, w_att
             shape = [P, HEADS, 2, HALF]
             for s, table, dst in ((0, with_lo, lo_prod), (1, with_hi, hi_prod)):
                 nc.vector.tensor_tensor(
-                    out=dst[:, :, j % PAIR, :].rearrange("p h (s d) -> p h s d", s=2),
+                    out=dst[:, :, jj, :].rearrange("p h (s d) -> p h s d", s=2),
                     in0=halves[:, :, s : s + 1, :].to_broadcast(shape),
                     in1=table.unsqueeze(1).to_broadcast(shape),
                     op=ALU.mult,
@@ -168,68 +172,81 @@ def tile_swaattention_pa_kernel(tc, x, freqs_cos, freqs_sin, w_attn_words, w_att
             h0 = (c % 2) * HEADS
             return outs[c // 2][:, h0 : h0 + HEADS, j * D : (j + count) * D]
 
-        def flat(t):
-            return t[:].rearrange("p h j d -> p (h j d)")
+        def tiles_of(t, jj, count):
+            return t[:, :, jj : jj + count, :].rearrange("p h j d -> p h (j d)")
+
+        def add(engine, rotated, jj, lo_prod, hi_prod, pj, count):
+            engine.tensor_tensor(
+                out=tiles_of(rotated, jj, count), in0=tiles_of(lo_prod, pj, count), in1=tiles_of(hi_prod, pj, count),
+                op=ALU.add,
+            )
+
+        def store(engine, t, c, j0, jj, count):
+            engine.dma_start(out=out_view(c, j0 + jj, count), in_=tiles_of(t, jj, count))
 
         banks0 = transpose_group(0)
         banks1 = transpose_group(1)
-        interleave(nc.vector.tensor_copy, 0, banks0)
+        interleave(nc.scalar.copy, 0, banks0)
         quantize(0)
         count = TABLE_GROUPS[0][1]
         nc.vector.tensor_scalar(
             out=tables[0][:, 0:count, :], in0=tables[0][:, 3 * count : 5 * count : 2, :],
             scalar1=-1.0, scalar2=None, op0=ALU.mult,
         )
-        interleave(nc.vector.tensor_copy, 1, banks1)
+        interleave(nc.scalar.copy, 1, banks1)
         quantize(1)
 
-        rot_steps = [(j0 + jj, c) for j0 in range(0, TILES, PAIR) for c in range(4) for jj in range(PAIR)]
-        v_steps = [(j0 + jj, c) for j0 in range(0, TILES, PAIR) for c in (4, 5) for jj in range(PAIR)]
+        rot_steps = [(j0, n, jj, c) for j0, n in OUT_GROUPS for c in range(4) for jj in range(n)]
+        v_steps = [(j0, n, jj, c) for j0, n in OUT_GROUPS for c in (4, 5) for jj in range(n)]
         v_done = 0
         v_res = None
-        lo_prod = hi_prod = None
-        for s, (j, c) in enumerate(rot_steps):
+        lo_prod = hi_prod = rotated = None
+        left = []
+        for s, (j0, n, jj, c) in enumerate(rot_steps):
             bank = rot_ps.tile([P, NCOL], F32, name="rot")
-            project(bank, j, c)
-            if j % PAIR == 0:
-                lo_prod = prod.tile([P, HEADS, PAIR, D], F32, name="lo_prod")
-                hi_prod = prod.tile([P, HEADS, PAIR, D], F32, name="hi_prod")
-            products(bank, j, lo_prod, hi_prod)
-            if j % PAIR == PAIR - 1:
-                j0 = j - (PAIR - 1)
-                rotated = res.tile([P, HEADS, PAIR, D], F32, name="rotated")
-                if s < len(rot_steps) - 1:
-                    nc.gpsimd.tensor_tensor(out=flat(rotated), in0=flat(lo_prod), in1=flat(hi_prod), op=ALU.add)
-                    nc.sync.dma_start(out=out_view(c, j0, PAIR), in_=rotated[:].rearrange("p h j d -> p h (j d)"))
-                else:
-                    for jj in range(PAIR):
-                        nc.vector.tensor_tensor(
-                            out=rotated[:, :, jj, :], in0=lo_prod[:, :, jj, :], in1=hi_prod[:, :, jj, :], op=ALU.add
-                        )
-                        nc.sync.dma_start(out=out_view(c, j0 + jj, 1), in_=rotated[:, :, jj, :])
+            project(bank, j0 + jj, c)
+            span = 1 if s < ADD_SPAN else ADD_SPAN
+            if jj % span == 0:
+                lo_prod = prod.tile([P, HEADS, span, D], F32, name="lo_prod")
+                hi_prod = prod.tile([P, HEADS, span, D], F32, name="hi_prod")
+            if jj == 0:
+                rotated = res.tile([P, HEADS, n, D], F32, name="rotated")
+            products(bank, j0 + jj, jj % span, lo_prod, hi_prod)
+            if s >= len(rot_steps) - VECTOR_ADDS:
+                if jj == n - 1:
+                    left.append((j0, n, c, lo_prod, hi_prod, rotated))
+            else:
+                if (jj + 1) % span == 0:
+                    add(nc.gpsimd, rotated, jj + 1 - span, lo_prod, hi_prod, 0, span)
+                if jj == n - 1:
+                    store(nc.sync, rotated, c, j0, 0, n)
 
-            if s in QUANTIZE_AFTER:
-                quantize(QUANTIZE_AFTER[s])
             if s in TRANSPOSE_AFTER:
-                n = TRANSPOSE_AFTER[s]
-                interleave(nc.scalar.copy, n, transpose_group(n))
-                if n == 2:
+                xn = TRANSPOSE_AFTER[s]
+                interleave(nc.scalar.copy, xn, transpose_group(xn))
+                if xn == 3:
                     count = TABLE_GROUPS[1][1]
                     nc.scalar.activation(
                         out=tables[1][:, 0:count, :], in_=tables[1][:, 3 * count : 5 * count : 2, :],
                         func=ACT.Copy, scale=-1.0,
                     )
+            if s in QUANTIZE_AFTER:
+                quantize(QUANTIZE_AFTER[s])
 
             v_due = 0 if s < V_FIRST else min(len(v_steps), (s - V_FIRST + 1) * len(v_steps) // (V_LAST - V_FIRST + 1))
             while v_done < v_due:
-                vj, vc = v_steps[v_done]
+                vj0, vn, vjj, vc = v_steps[v_done]
                 v_done += 1
                 v_bank = aux_ps.tile([P, NCOL], F32, name="aux")
-                project(v_bank, vj, vc)
-                if vj % PAIR == 0:
-                    v_res = res.tile([P, HEADS, PAIR, D], F32, name="v_res")
-                nc.scalar.copy(out=v_res[:, :, vj % PAIR, :], in_=v_bank[:].rearrange("p (h d) -> p h d", d=D))
-                if vj % PAIR == PAIR - 1:
-                    nc.scalar.dma_start(
-                        out=out_view(vc, vj - (PAIR - 1), PAIR), in_=v_res[:].rearrange("p h j d -> p h (j d)")
-                    )
+                project(v_bank, vj0 + vjj, vc)
+                if vjj == 0:
+                    v_res = v_pool.tile([P, HEADS, vn, D], F32, name="v_res")
+                nc.scalar.copy(out=v_res[:, :, vjj, :], in_=v_bank[:].rearrange("p (h d) -> p h d", d=D))
+                if vjj == vn - 1:
+                    store(nc.scalar, v_res, vc, vj0, 0, vn)
+
+        for i, (j0, n, c, lo_prod, hi_prod, rotated) in enumerate(left):
+            span = n if i < len(left) - 1 else 1
+            for jj in range(0, n, span):
+                add(nc.vector, rotated, jj, lo_prod, hi_prod, jj, span)
+                store(nc.sync, rotated, c, j0, jj, span)

@@ -19,19 +19,18 @@ ACT = mybir.ActivationFunctionType
 
 P = 128
 TILES = T // P
-PASSES = C // 512
+KPASS = 512
+PASSES = C // KPASS
 NCOL = 512
 HEADS = NCOL // D
 
-X_GROUPS = [(0, 1), (1, 1), (2, 2), (4, 2), (6, 4), (10, 2)]
-OUT_GROUPS = [(0, 2), (2, 4), (6, 4), (10, 2)]
+X_PIECES = [(0, 1, 0, 1), (0, 1, 1, 1), (1, 1, 0, 2), (2, 2, 0, 2), (4, 4, 0, 2), (8, 4, 0, 2)]
+PAIR = 2
 TABLE_GROUPS = [(0, 2), (2, 10)]
 W_GROUPS = [(0, 1), (1, 1), (2, 2), (4, 2)]
 PLANE_GROUPS = [(0, 2), (2, 4)]
-TRANSPOSE_AFTER = {3: 2, 7: 3, 10: 4, 13: 5}
-QUANTIZE_AFTER = {5: 2, 7: 3, 11: 4, 15: 5}
-V_FIRST, V_LAST = 11, 42
-ADD_SPAN = 2
+PREPARE_AFTER = {3: 3, 11: 4, 13: 5}
+V_FIRST, V_LAST = 12, 40
 VECTOR_ADDS = 6
 
 
@@ -42,9 +41,16 @@ def group_of(groups, i):
     raise ValueError(i)
 
 
+def codes_of(j, g):
+    for n, (first, count, g0, gn) in enumerate(X_PIECES):
+        if first <= j < first + count and g0 <= g < g0 + gn:
+            return n, ((j - first) * gn + g - g0) * P
+    raise ValueError(j)
+
+
 def tile_swaattention_pa_kernel(tc, x, freqs_cos, freqs_sin, w_attn_words, w_attn_scales, out_0, out_1, out_2):
     nc = tc.nc
-    x_rows = x[0].rearrange("(p j) c -> p (j c)", j=TILES)
+    x_rows = x[0].rearrange("(p j) c -> p j c", j=TILES)
     cos_rows = freqs_cos.rearrange("(p j) d -> p (j d)", j=TILES)
     sin_rows = freqs_sin.rearrange("(p j) d -> p (j d)", j=TILES)
     w_rows = w_attn_words.rearrange("g p n -> p g n")
@@ -53,20 +59,23 @@ def tile_swaattention_pa_kernel(tc, x, freqs_cos, freqs_sin, w_attn_words, w_att
     with ExitStack() as ctx:
         keep = ctx.enter_context(tc.tile_pool(name="keep", bufs=1))
         prod = ctx.enter_context(tc.tile_pool(name="prod", bufs=6))
-        res = ctx.enter_context(tc.tile_pool(name="res", bufs=5))
-        v_pool = ctx.enter_context(tc.tile_pool(name="v_pool", bufs=4))
-        rot_ps = ctx.enter_context(tc.psum_pool(name="rot_ps", bufs=4))
-        aux_ps = ctx.enter_context(tc.psum_pool(name="aux_ps", bufs=4))
+        res = ctx.enter_context(tc.tile_pool(name="res", bufs=9))
+        v_pool = ctx.enter_context(tc.tile_pool(name="v_pool", bufs=7))
+        rot_ps = ctx.enter_context(tc.psum_pool(name="rot_ps", bufs=5))
+        aux_ps = ctx.enter_context(tc.psum_pool(name="aux_ps", bufs=3))
         ctx.enter_context(tc.manual_schedule())
 
         ident = keep.tile([P, P], F32, name="ident")
         make_identity(nc, ident[:])
 
-        x_sb = [keep.tile([P, n * C], BF16, name="x%d" % f, align_bytes=64) for f, n in X_GROUPS]
-        grouped = [keep.tile([P, n * C], BF16, name="grouped%d" % f, align_bytes=64) for f, n in X_GROUPS]
-        codes = [keep.tile([P, n * C // 4], U32, name="codes%d" % f, align_bytes=64) for f, n in X_GROUPS]
-        scales = [keep.tile([P, n * C // 4], U8, name="scales%d" % f, align_bytes=64) for f, n in X_GROUPS]
-        tables = [keep.tile([P, 5 * n, HALF], BF16, name="tables%d" % f, align_bytes=64) for f, n in TABLE_GROUPS]
+        widths = [n * gn * KPASS for f, n, g0, gn in X_PIECES]
+        x_sb = [keep.tile([P, w], BF16, name="x%d" % i, align_bytes=64) for i, w in enumerate(widths)]
+        grouped = [keep.tile([P, w], BF16, name="grouped%d" % i, align_bytes=64) for i, w in enumerate(widths)]
+        codes = [keep.tile([P, w // 4], U32, name="codes%d" % i, align_bytes=64) for i, w in enumerate(widths)]
+        scales = [keep.tile([P, w // 4], U8, name="scales%d" % i, align_bytes=64) for i, w in enumerate(widths)]
+        cos_sb = [keep.tile([P, n, 2, HALF], BF16, name="cos%d" % f, align_bytes=64) for f, n in TABLE_GROUPS]
+        sin_sb = [keep.tile([P, n, 2, HALF], BF16, name="sin%d" % f, align_bytes=64) for f, n in TABLE_GROUPS]
+        factors = [keep.tile([P, n, 4, HALF], BF16, name="factors%d" % f, align_bytes=64) for f, n in TABLE_GROUPS]
         w_sb = [keep.tile([P, PASSES, n * 2 * NCOL], U8, name="w%d" % f, align_bytes=64) for f, n in W_GROUPS]
         planes = [keep.tile([P, PASSES, n * NCOL], U8, name="plane%d" % f, align_bytes=64) for f, n in PLANE_GROUPS]
 
@@ -74,8 +83,11 @@ def tile_swaattention_pa_kernel(tc, x, freqs_cos, freqs_sin, w_attn_words, w_att
             nc.vector.memset(plane[:].bitcast(I32), 0)
 
         def load_x(n):
-            first, count = X_GROUPS[n]
-            nc.sync.dma_start(out=x_sb[n][:], in_=x_rows[:, first * C : (first + count) * C])
+            first, count, g0, gn = X_PIECES[n]
+            nc.sync.dma_start(
+                out=x_sb[n][:].rearrange("p (j c) -> p j c", j=count),
+                in_=x_rows[:, first : first + count, g0 * KPASS : (g0 + gn) * KPASS],
+            )
 
         def load_w(n):
             first, count = W_GROUPS[n]
@@ -94,54 +106,48 @@ def tile_swaattention_pa_kernel(tc, x, freqs_cos, freqs_sin, w_attn_words, w_att
         def load_tables(n):
             first, count = TABLE_GROUPS[n]
             cols = slice(first * D, (first + count) * D)
-            flat = tables[n][:].rearrange("p b d -> p (b d)")
-            nc.sync.dma_start(out=flat[:, count * HALF : 3 * count * HALF], in_=cos_rows[:, cols])
-            nc.sync.dma_start(out=flat[:, 3 * count * HALF : 5 * count * HALF], in_=sin_rows[:, cols])
+            nc.sync.dma_start(out=cos_sb[n][:].rearrange("p j s d -> p (j s d)"), in_=cos_rows[:, cols])
+            nc.sync.dma_start(out=sin_sb[n][:].rearrange("p j s d -> p (j s d)"), in_=sin_rows[:, cols])
 
         load_x(0)
         load_x(1)
+        load_x(2)
         load_w(0)
         load_plane(0)
         load_tables(0)
         load_w(1)
-        load_x(2)
+        load_x(3)
         load_plane(1)
         load_w(2)
-        load_x(3)
         load_tables(1)
         load_x(4)
         load_w(3)
         load_x(5)
 
-        def transpose_group(n):
-            banks = []
-            for jj in range(X_GROUPS[n][1]):
-                words = x_sb[n][:, jj * C : (jj + 1) * C].bitcast(F32)
+        def transpose_piece(n):
+            first, count, g0, gn = X_PIECES[n]
+            width = gn * KPASS
+            for jj in range(count):
+                words = x_sb[n][:, jj * width : (jj + 1) * width].bitcast(F32)
                 bank = aux_ps.tile([P, NCOL], F32, name="aux")
-                for g in range(PASSES):
+                for g in range(gn):
                     for u in range(2):
                         col = (2 * g + u) * P
                         nc.tensor.transpose(bank[:, col : col + P], words[:, 256 * g + u : 256 * (g + 1) : 2], ident[:])
-                banks.append(bank)
-            return banks
-
-        def interleave(copy, n, banks):
-            for jj, bank in enumerate(banks):
-                dst = grouped[n][:, jj * C : (jj + 1) * C].bitcast(F32)
-                copy(
-                    out=dst.rearrange("p (g r u) -> p g r u", g=PASSES, u=2),
-                    in_=bank[:].rearrange("p (g u r) -> p g r u", g=PASSES, u=2),
+                dst = grouped[n][:, jj * width : (jj + 1) * width].bitcast(F32)
+                nc.scalar.copy(
+                    out=dst.rearrange("p (g r u) -> p g r u", g=gn, u=2),
+                    in_=bank[:, 0 : gn * 2 * P].rearrange("p (g u r) -> p g r u", g=gn, u=2),
                 )
 
         def quantize(n):
             nc.vector.quantize_mx(out=codes[n][:].bitcast(E5M2X4), scales=scales[n][:], in_=grouped[n][:])
 
         def project(bank, j, c):
-            xn, jj = group_of(X_GROUPS, j)
             wn, wc = group_of(W_GROUPS, c)
             pn, pc = group_of(PLANE_GROUPS, c)
             for g in range(PASSES):
-                col = (jj * PASSES + g) * P
+                xn, col = codes_of(j, g)
                 nc.tensor.matmul_mx(
                     out=bank[:],
                     lhsT=codes[xn][:, col : col + P].bitcast(E5M2X4),
@@ -152,21 +158,15 @@ def tile_swaattention_pa_kernel(tc, x, freqs_cos, freqs_sin, w_attn_words, w_att
                     stop=(g == PASSES - 1),
                 )
 
-        def products(bank, j, jj, lo_prod, hi_prod):
+        def products(bank, j, both, jj):
             tn, tj = group_of(TABLE_GROUPS, j)
-            count = TABLE_GROUPS[tn][1]
-            neg_sin_lo, cos_lo, sin_lo = tj, count + 2 * tj, 3 * count + 2 * tj
-            with_lo = tables[tn][:, cos_lo : sin_lo + 2 : sin_lo + 1 - cos_lo, :]
-            with_hi = tables[tn][:, neg_sin_lo : cos_lo + 2 : cos_lo + 1 - neg_sin_lo, :]
-            halves = bank[:].rearrange("p (h s d) -> p h s d", s=2, d=HALF)
-            shape = [P, HEADS, 2, HALF]
-            for s, table, dst in ((0, with_lo, lo_prod), (1, with_hi, hi_prod)):
-                nc.vector.tensor_tensor(
-                    out=dst[:, :, jj, :].rearrange("p h (s d) -> p h s d", s=2),
-                    in0=halves[:, :, s : s + 1, :].to_broadcast(shape),
-                    in1=table.unsqueeze(1).to_broadcast(shape),
-                    op=ALU.mult,
-                )
+            shape = [P, HEADS, 2, 2, HALF]
+            nc.vector.tensor_tensor(
+                out=both[:, :, jj, :, :].rearrange("p h s (o d) -> p h s o d", o=2),
+                in0=bank[:].rearrange("p (h s o d) -> p h s o d", s=2, o=1, d=HALF).to_broadcast(shape),
+                in1=factors[tn][:, tj : tj + 1, :, :].rearrange("p j (s o) d -> p j s o d", s=2).to_broadcast(shape),
+                op=ALU.mult,
+            )
 
         def out_view(c, j, count):
             h0 = (c % 2) * HEADS
@@ -175,78 +175,78 @@ def tile_swaattention_pa_kernel(tc, x, freqs_cos, freqs_sin, w_attn_words, w_att
         def tiles_of(t, jj, count):
             return t[:, :, jj : jj + count, :].rearrange("p h j d -> p h (j d)")
 
-        def add(engine, rotated, jj, lo_prod, hi_prod, pj, count):
+        def add(engine, rotated, jj, both, pj, count):
             engine.tensor_tensor(
-                out=tiles_of(rotated, jj, count), in0=tiles_of(lo_prod, pj, count), in1=tiles_of(hi_prod, pj, count),
+                out=rotated[:, :, jj : jj + count, :],
+                in0=both[:, :, pj : pj + count, 0, :],
+                in1=both[:, :, pj : pj + count, 1, :],
                 op=ALU.add,
             )
 
         def store(engine, t, c, j0, jj, count):
             engine.dma_start(out=out_view(c, j0 + jj, count), in_=tiles_of(t, jj, count))
 
-        banks0 = transpose_group(0)
-        banks1 = transpose_group(1)
-        interleave(nc.scalar.copy, 0, banks0)
+        transpose_piece(0)
         quantize(0)
-        count = TABLE_GROUPS[0][1]
-        nc.vector.tensor_scalar(
-            out=tables[0][:, 0:count, :], in0=tables[0][:, 3 * count : 5 * count : 2, :],
-            scalar1=-1.0, scalar2=None, op0=ALU.mult,
-        )
-        interleave(nc.scalar.copy, 1, banks1)
+        transpose_piece(1)
         quantize(1)
+        nc.vector.tensor_copy(out=factors[0][:, :, 0:4:3, :], in_=cos_sb[0][:])
+        nc.vector.tensor_copy(out=factors[0][:, :, 1, :], in_=sin_sb[0][:, :, 1, :])
+        nc.vector.tensor_scalar(
+            out=factors[0][:, :, 2, :], in0=sin_sb[0][:, :, 0, :], scalar1=-1.0, scalar2=None, op0=ALU.mult
+        )
+        transpose_piece(2)
+        quantize(2)
 
-        rot_steps = [(j0, n, jj, c) for j0, n in OUT_GROUPS for c in range(4) for jj in range(n)]
-        v_steps = [(j0, n, jj, c) for j0, n in OUT_GROUPS for c in (4, 5) for jj in range(n)]
+        rot_steps = [(j0, jj, c) for j0 in range(0, TILES, PAIR) for c in range(4) for jj in range(PAIR)]
+        v_steps = [(j0, jj, c) for j0 in range(0, TILES, PAIR) for c in (4, 5) for jj in range(PAIR)]
         v_done = 0
-        v_res = None
-        lo_prod = hi_prod = rotated = None
+        both = rotated = v_res = None
         left = []
-        for s, (j0, n, jj, c) in enumerate(rot_steps):
+        for s, (j0, jj, c) in enumerate(rot_steps):
             bank = rot_ps.tile([P, NCOL], F32, name="rot")
             project(bank, j0 + jj, c)
-            span = 1 if s < ADD_SPAN else ADD_SPAN
+            span = 1 if s < PAIR else PAIR
             if jj % span == 0:
-                lo_prod = prod.tile([P, HEADS, span, D], F32, name="lo_prod")
-                hi_prod = prod.tile([P, HEADS, span, D], F32, name="hi_prod")
-            if jj == 0:
-                rotated = res.tile([P, HEADS, n, D], F32, name="rotated")
-            products(bank, j0 + jj, jj % span, lo_prod, hi_prod)
+                both = prod.tile([P, HEADS, span, 2, D], F32, name="both")
+            products(bank, j0 + jj, both, jj % span)
             if s >= len(rot_steps) - VECTOR_ADDS:
-                if jj == n - 1:
-                    left.append((j0, n, c, lo_prod, hi_prod, rotated))
+                if jj == PAIR - 1:
+                    left.append((j0, c, both))
             else:
+                if jj == 0:
+                    rotated = res.tile([P, HEADS, PAIR, D], F32, name="rotated")
                 if (jj + 1) % span == 0:
-                    add(nc.gpsimd, rotated, jj + 1 - span, lo_prod, hi_prod, 0, span)
-                if jj == n - 1:
-                    store(nc.sync, rotated, c, j0, 0, n)
+                    add(nc.gpsimd, rotated, jj + 1 - span, both, 0, span)
+                if jj == PAIR - 1:
+                    store(nc.sync, rotated, c, j0, 0, PAIR)
 
-            if s in TRANSPOSE_AFTER:
-                xn = TRANSPOSE_AFTER[s]
-                interleave(nc.scalar.copy, xn, transpose_group(xn))
+            if s in PREPARE_AFTER:
+                xn = PREPARE_AFTER[s]
+                transpose_piece(xn)
+                quantize(xn)
                 if xn == 3:
-                    count = TABLE_GROUPS[1][1]
+                    nc.scalar.copy(out=factors[1][:, :, 0:4:3, :], in_=cos_sb[1][:])
+                    nc.scalar.copy(out=factors[1][:, :, 1, :], in_=sin_sb[1][:, :, 1, :])
                     nc.scalar.activation(
-                        out=tables[1][:, 0:count, :], in_=tables[1][:, 3 * count : 5 * count : 2, :],
-                        func=ACT.Copy, scale=-1.0,
+                        out=factors[1][:, :, 2, :], in_=sin_sb[1][:, :, 0, :], func=ACT.Copy, scale=-1.0
                     )
-            if s in QUANTIZE_AFTER:
-                quantize(QUANTIZE_AFTER[s])
 
-            v_due = 0 if s < V_FIRST else min(len(v_steps), (s - V_FIRST + 1) * len(v_steps) // (V_LAST - V_FIRST + 1))
+            v_due = min(len(v_steps), max(0, (s - V_FIRST + 1) * len(v_steps) // (V_LAST - V_FIRST + 1)))
             while v_done < v_due:
-                vj0, vn, vjj, vc = v_steps[v_done]
+                vj0, vjj, vc = v_steps[v_done]
                 v_done += 1
                 v_bank = aux_ps.tile([P, NCOL], F32, name="aux")
                 project(v_bank, vj0 + vjj, vc)
                 if vjj == 0:
-                    v_res = v_pool.tile([P, HEADS, vn, D], F32, name="v_res")
+                    v_res = v_pool.tile([P, HEADS, PAIR, D], F32, name="v_res")
                 nc.scalar.copy(out=v_res[:, :, vjj, :], in_=v_bank[:].rearrange("p (h d) -> p h d", d=D))
-                if vjj == vn - 1:
-                    store(nc.scalar, v_res, vc, vj0, 0, vn)
+                if vjj == PAIR - 1:
+                    store(nc.scalar, v_res, vc, vj0, 0, PAIR)
 
-        for i, (j0, n, c, lo_prod, hi_prod, rotated) in enumerate(left):
-            span = n if i < len(left) - 1 else 1
-            for jj in range(0, n, span):
-                add(nc.vector, rotated, jj, lo_prod, hi_prod, jj, span)
-                store(nc.sync, rotated, c, j0, jj, span)
+        for i, (j0, c, both) in enumerate(left):
+            span = PAIR if i < len(left) - 1 else 1
+            for jj in range(0, PAIR, span):
+                rotated = res.tile([P, HEADS, span, D], F32, name="rotated")
+                add(nc.vector, rotated, 0, both, jj, span)
+                store(nc.sync, rotated, c, j0 + jj, 0, span)

@@ -26,12 +26,18 @@ HEADS = NCOL // D
 
 X_PIECES = [(0, 1, 0, 1), (0, 1, 1, 1), (1, 1, 0, 2), (2, 2, 0, 2), (4, 4, 0, 2), (8, 4, 0, 2)]
 PAIR = 2
+ORDER_GROUPS = [(0, 2), (2, 2), (4, 4), (8, 4)]
+STORE_GROUPS = [(0, 2), (2, 2), (4, 4), (8, 4)]
+V_GROUPS = [(0, 4), (4, 4), (8, 4)]
 TABLE_GROUPS = [(0, 2), (2, 10)]
 W_GROUPS = [(0, 1), (1, 1), (2, 2), (4, 2)]
 PLANE_GROUPS = [(0, 2), (2, 4)]
 PREPARE_AFTER = {3: 3, 11: 4, 13: 5}
 V_FIRST, V_LAST = 12, 40
-VECTOR_ADDS = 6
+VECTOR_ADDS_AT = (29,)
+HOLD = 2
+SPLIT_LAST = 1
+TAILH = 1
 
 
 def group_of(groups, i):
@@ -58,9 +64,9 @@ def tile_swaattention_pa_kernel(tc, x, freqs_cos, freqs_sin, w_attn_words, w_att
 
     with ExitStack() as ctx:
         keep = ctx.enter_context(tc.tile_pool(name="keep", bufs=1))
-        prod = ctx.enter_context(tc.tile_pool(name="prod", bufs=6))
-        res = ctx.enter_context(tc.tile_pool(name="res", bufs=9))
-        v_pool = ctx.enter_context(tc.tile_pool(name="v_pool", bufs=7))
+        prod = ctx.enter_context(tc.tile_pool(name="prod", bufs=5))
+        res = ctx.enter_context(tc.tile_pool(name="res", bufs=6))
+        v_pool = ctx.enter_context(tc.tile_pool(name="v_pool", bufs=4))
         rot_ps = ctx.enter_context(tc.psum_pool(name="rot_ps", bufs=5))
         aux_ps = ctx.enter_context(tc.psum_pool(name="aux_ps", bufs=3))
         ctx.enter_context(tc.manual_schedule())
@@ -198,28 +204,46 @@ def tile_swaattention_pa_kernel(tc, x, freqs_cos, freqs_sin, w_attn_words, w_att
         transpose_piece(2)
         quantize(2)
 
-        rot_steps = [(j0, jj, c) for j0 in range(0, TILES, PAIR) for c in range(4) for jj in range(PAIR)]
-        v_steps = [(j0, jj, c) for j0 in range(0, TILES, PAIR) for c in (4, 5) for jj in range(PAIR)]
+        rot_steps = [(j0 + jj, c) for j0, n in ORDER_GROUPS for c in range(4) for jj in range(n)]
+        v_steps = [(j0, n, jj, c) for j0, n in V_GROUPS for c in (4, 5) for jj in range(n)]
+        last_first, last_count = ORDER_GROUPS[-1]
+        tail_start = len(rot_steps) - last_count
+
+        def store_group(j, c):
+            first, count = STORE_GROUPS[group_of(STORE_GROUPS, j)[0]]
+            if first == last_first and c >= 3 - SPLIT_LAST:
+                return j - j % PAIR, PAIR
+            return first, count
+
+        def add_and_store(engine, j, c, both, span):
+            first, count = store_group(j, c)
+            if j + 1 - span == first:
+                rotated[c] = res.tile([P, HEADS, count, D], F32, name="rotated")
+            add(engine, rotated[c], j + 1 - span - first, both, 0, span)
+            if j + 1 == first + count:
+                store(nc.sync, rotated[c], c, first, 0, count)
+
         v_done = 0
-        both = rotated = v_res = None
-        left = []
-        for s, (j0, jj, c) in enumerate(rot_steps):
+        both = v_res = None
+        rotated = {}
+        held = {}
+        for s, (j, c) in enumerate(rot_steps):
             bank = rot_ps.tile([P, NCOL], F32, name="rot")
-            project(bank, j0 + jj, c)
-            span = 1 if s < PAIR else PAIR
-            if jj % span == 0:
-                both = prod.tile([P, HEADS, span, 2, D], F32, name="both")
-            products(bank, j0 + jj, both, jj % span)
-            if s >= len(rot_steps) - VECTOR_ADDS:
-                if jj == PAIR - 1:
-                    left.append((j0, c, both))
-            else:
-                if jj == 0:
-                    rotated = res.tile([P, HEADS, PAIR, D], F32, name="rotated")
-                if (jj + 1) % span == 0:
-                    add(nc.gpsimd, rotated, jj + 1 - span, both, 0, span)
-                if jj == PAIR - 1:
-                    store(nc.sync, rotated, c, j0, 0, PAIR)
+            project(bank, j, c)
+            span = 1 if s < PAIR else PAIR if s < tail_start else last_count
+            if (j - last_first) % span == 0:
+                if s < tail_start:
+                    both = prod.tile([P, HEADS, span, 2, D], F32, name="both")
+                else:
+                    both = keep.tile([P, HEADS, span, 2, D], F32, name="both_last")
+            products(bank, j, both, (j - last_first) % span)
+            if s in held:
+                add_and_store(nc.vector, *held[s])
+            if (j + 1) % span == 0 and s < tail_start:
+                if s in VECTOR_ADDS_AT:
+                    held[s + HOLD] = (j, c, both, span)
+                else:
+                    add_and_store(nc.gpsimd, j, c, both, span)
 
             if s in PREPARE_AFTER:
                 xn = PREPARE_AFTER[s]
@@ -234,19 +258,22 @@ def tile_swaattention_pa_kernel(tc, x, freqs_cos, freqs_sin, w_attn_words, w_att
 
             v_due = min(len(v_steps), max(0, (s - V_FIRST + 1) * len(v_steps) // (V_LAST - V_FIRST + 1)))
             while v_done < v_due:
-                vj0, vjj, vc = v_steps[v_done]
+                vj0, vn, vjj, vc = v_steps[v_done]
                 v_done += 1
                 v_bank = aux_ps.tile([P, NCOL], F32, name="aux")
                 project(v_bank, vj0 + vjj, vc)
                 if vjj == 0:
-                    v_res = v_pool.tile([P, HEADS, PAIR, D], F32, name="v_res")
+                    v_res = v_pool.tile([P, HEADS, vn, D], F32, name="v_res")
                 nc.scalar.copy(out=v_res[:, :, vjj, :], in_=v_bank[:].rearrange("p (h d) -> p h d", d=D))
-                if vjj == PAIR - 1:
-                    store(nc.scalar, v_res, vc, vj0, 0, PAIR)
+                if vjj == vn - 1:
+                    store(nc.scalar, v_res, vc, vj0, 0, vn)
 
-        for i, (j0, c, both) in enumerate(left):
-            span = PAIR if i < len(left) - 1 else 1
-            for jj in range(0, PAIR, span):
-                rotated = res.tile([P, HEADS, span, D], F32, name="rotated")
-                add(nc.vector, rotated, 0, both, jj, span)
-                store(nc.sync, rotated, c, j0 + jj, 0, span)
+        for h in range(0, HEADS, TAILH):
+            last = res.tile([P, TAILH, last_count, D], F32, name="rotated")
+            nc.vector.tensor_tensor(
+                out=last[:], in0=both[:, h : h + TAILH, :, 0, :], in1=both[:, h : h + TAILH, :, 1, :], op=ALU.add
+            )
+            nc.sync.dma_start(
+                out=outs[1][:, HEADS + h : HEADS + h + TAILH, last_first * D : TILES * D],
+                in_=last[:].rearrange("p h j d -> p h (j d)"),
+            )

from contextlib import ExitStack

import concourse.mybir as mybir
from concourse.masks import make_identity

T, C, H, D = 1536, 1024, 8, 128
HALF = D // 2
FLOPS = 2 * T * C * 3 * C

F32 = mybir.dt.float32
BF16 = mybir.dt.bfloat16
I32 = mybir.dt.int32
U32 = mybir.dt.uint32
U8 = mybir.dt.uint8
E5M2X4 = mybir.dt.float8_e5m2_x4
E2M1X4 = mybir.dt.float4_e2m1fn_x4
ALU = mybir.AluOpType
ACT = mybir.ActivationFunctionType

P = 128
TILES = T // P
KPASS = 512
PASSES = C // KPASS
NCOL = 512
HEADS = NCOL // D

X_PIECES = [(0, 1, 0, 1), (0, 1, 1, 1), (1, 1, 0, 2), (2, 2, 0, 2), (4, 4, 0, 2), (8, 4, 0, 2)]
PAIR = 2
ORDER_GROUPS = [(0, 2), (2, 2), (4, 4), (8, 4)]
STORE_GROUPS = [(0, 2), (2, 2), (4, 4), (8, 4)]
V_GROUPS = [(0, 4), (4, 4), (8, 4)]
TABLE_GROUPS = [(0, 2), (2, 10)]
W_GROUPS = [(0, 1), (1, 1), (2, 2), (4, 2)]
PLANE_GROUPS = [(0, 2), (2, 4)]
PREPARE_AFTER = {3: 3, 11: 4, 13: 5}
V_FIRST, V_LAST = 12, 40
VECTOR_ADDS_AT = (29,)
HOLD = 2
SPLIT_LAST = 1
TAILH = 1


def group_of(groups, i):
    for n, (first, count) in enumerate(groups):
        if first <= i < first + count:
            return n, i - first
    raise ValueError(i)


def codes_of(j, g):
    for n, (first, count, g0, gn) in enumerate(X_PIECES):
        if first <= j < first + count and g0 <= g < g0 + gn:
            return n, ((j - first) * gn + g - g0) * P
    raise ValueError(j)


def tile_swaattention_pa_kernel(tc, x, freqs_cos, freqs_sin, w_attn_words, w_attn_scales, out_0, out_1, out_2):
    nc = tc.nc
    x_rows = x[0].rearrange("(p j) c -> p j c", j=TILES)
    cos_rows = freqs_cos.rearrange("(p j) d -> p (j d)", j=TILES)
    sin_rows = freqs_sin.rearrange("(p j) d -> p (j d)", j=TILES)
    w_rows = w_attn_words.rearrange("g p n -> p g n")
    outs = [o[0].rearrange("h (p j) d -> p h (j d)", j=TILES) for o in (out_0, out_1, out_2)]

    with ExitStack() as ctx:
        keep = ctx.enter_context(tc.tile_pool(name="keep", bufs=1))
        prod = ctx.enter_context(tc.tile_pool(name="prod", bufs=5))
        res = ctx.enter_context(tc.tile_pool(name="res", bufs=6))
        v_pool = ctx.enter_context(tc.tile_pool(name="v_pool", bufs=4))
        rot_ps = ctx.enter_context(tc.psum_pool(name="rot_ps", bufs=5))
        aux_ps = ctx.enter_context(tc.psum_pool(name="aux_ps", bufs=3))
        ctx.enter_context(tc.manual_schedule())

        ident = keep.tile([P, P], F32, name="ident")
        make_identity(nc, ident[:])

        widths = [n * gn * KPASS for f, n, g0, gn in X_PIECES]
        x_sb = [keep.tile([P, w], BF16, name="x%d" % i, align_bytes=64) for i, w in enumerate(widths)]
        grouped = [keep.tile([P, w], BF16, name="grouped%d" % i, align_bytes=64) for i, w in enumerate(widths)]
        codes = [keep.tile([P, w // 4], U32, name="codes%d" % i, align_bytes=64) for i, w in enumerate(widths)]
        scales = [keep.tile([P, w // 4], U8, name="scales%d" % i, align_bytes=64) for i, w in enumerate(widths)]
        cos_sb = [keep.tile([P, n, 2, HALF], BF16, name="cos%d" % f, align_bytes=64) for f, n in TABLE_GROUPS]
        sin_sb = [keep.tile([P, n, 2, HALF], BF16, name="sin%d" % f, align_bytes=64) for f, n in TABLE_GROUPS]
        factors = [keep.tile([P, n, 4, HALF], BF16, name="factors%d" % f, align_bytes=64) for f, n in TABLE_GROUPS]
        w_sb = [keep.tile([P, PASSES, n * 2 * NCOL], U8, name="w%d" % f, align_bytes=64) for f, n in W_GROUPS]
        planes = [keep.tile([P, PASSES, n * NCOL], U8, name="plane%d" % f, align_bytes=64) for f, n in PLANE_GROUPS]

        for plane in planes:
            nc.vector.memset(plane[:].bitcast(I32), 0)

        def load_x(n):
            first, count, g0, gn = X_PIECES[n]
            nc.sync.dma_start(
                out=x_sb[n][:].rearrange("p (j c) -> p j c", j=count),
                in_=x_rows[:, first : first + count, g0 * KPASS : (g0 + gn) * KPASS],
            )

        def load_w(n):
            first, count = W_GROUPS[n]
            cols = slice(first * 2 * NCOL, (first + count) * 2 * NCOL)
            nc.sync.dma_start(out=w_sb[n][:].bitcast(I32), in_=w_rows[:, :, cols].bitcast(I32))

        def load_plane(n):
            first, count = PLANE_GROUPS[n]
            cols = slice(first * NCOL, (first + count) * NCOL)
            for q in range(4):
                nc.sync.dma_start(
                    out=planes[n][32 * q : 32 * q + 4, :, :].bitcast(I32),
                    in_=w_attn_scales[:, 4 * q : 4 * q + 4, cols].rearrange("g r n -> r g n").bitcast(I32),
                )

        def load_tables(n):
            first, count = TABLE_GROUPS[n]
            cols = slice(first * D, (first + count) * D)
            nc.sync.dma_start(out=cos_sb[n][:].rearrange("p j s d -> p (j s d)"), in_=cos_rows[:, cols])
            nc.sync.dma_start(out=sin_sb[n][:].rearrange("p j s d -> p (j s d)"), in_=sin_rows[:, cols])

        load_x(0)
        load_x(1)
        load_x(2)
        load_w(0)
        load_plane(0)
        load_tables(0)
        load_w(1)
        load_x(3)
        load_plane(1)
        load_w(2)
        load_tables(1)
        load_x(4)
        load_w(3)
        load_x(5)

        def transpose_piece(n):
            first, count, g0, gn = X_PIECES[n]
            width = gn * KPASS
            for jj in range(count):
                words = x_sb[n][:, jj * width : (jj + 1) * width].bitcast(F32)
                bank = aux_ps.tile([P, NCOL], F32, name="aux")
                for g in range(gn):
                    for u in range(2):
                        col = (2 * g + u) * P
                        nc.tensor.transpose(bank[:, col : col + P], words[:, 256 * g + u : 256 * (g + 1) : 2], ident[:])
                dst = grouped[n][:, jj * width : (jj + 1) * width].bitcast(F32)
                nc.scalar.copy(
                    out=dst.rearrange("p (g r u) -> p g r u", g=gn, u=2),
                    in_=bank[:, 0 : gn * 2 * P].rearrange("p (g u r) -> p g r u", g=gn, u=2),
                )

        def quantize(n):
            nc.vector.quantize_mx(out=codes[n][:].bitcast(E5M2X4), scales=scales[n][:], in_=grouped[n][:])

        def project(bank, j, c):
            wn, wc = group_of(W_GROUPS, c)
            pn, pc = group_of(PLANE_GROUPS, c)
            for g in range(PASSES):
                xn, col = codes_of(j, g)
                nc.tensor.matmul_mx(
                    out=bank[:],
                    lhsT=codes[xn][:, col : col + P].bitcast(E5M2X4),
                    lhsT_scale=scales[xn][:, col : col + P],
                    rhs=w_sb[wn][:, g, wc * 2 * NCOL : (wc + 1) * 2 * NCOL].bitcast(E2M1X4),
                    rhs_scale=planes[pn][:, g, pc * NCOL : (pc + 1) * NCOL],
                    start=(g == 0),
                    stop=(g == PASSES - 1),
                )

        def products(bank, j, both, jj):
            tn, tj = group_of(TABLE_GROUPS, j)
            shape = [P, HEADS, 2, 2, HALF]
            nc.vector.tensor_tensor(
                out=both[:, :, jj, :, :].rearrange("p h s (o d) -> p h s o d", o=2),
                in0=bank[:].rearrange("p (h s o d) -> p h s o d", s=2, o=1, d=HALF).to_broadcast(shape),
                in1=factors[tn][:, tj : tj + 1, :, :].rearrange("p j (s o) d -> p j s o d", s=2).to_broadcast(shape),
                op=ALU.mult,
            )

        def out_view(c, j, count):
            h0 = (c % 2) * HEADS
            return outs[c // 2][:, h0 : h0 + HEADS, j * D : (j + count) * D]

        def tiles_of(t, jj, count):
            return t[:, :, jj : jj + count, :].rearrange("p h j d -> p h (j d)")

        def add(engine, rotated, jj, both, pj, count):
            engine.tensor_tensor(
                out=rotated[:, :, jj : jj + count, :],
                in0=both[:, :, pj : pj + count, 0, :],
                in1=both[:, :, pj : pj + count, 1, :],
                op=ALU.add,
            )

        def store(engine, t, c, j0, jj, count):
            engine.dma_start(out=out_view(c, j0 + jj, count), in_=tiles_of(t, jj, count))

        transpose_piece(0)
        quantize(0)
        transpose_piece(1)
        quantize(1)
        nc.vector.tensor_copy(out=factors[0][:, :, 0:4:3, :], in_=cos_sb[0][:])
        nc.vector.tensor_copy(out=factors[0][:, :, 1, :], in_=sin_sb[0][:, :, 1, :])
        nc.vector.tensor_scalar(
            out=factors[0][:, :, 2, :], in0=sin_sb[0][:, :, 0, :], scalar1=-1.0, scalar2=None, op0=ALU.mult
        )
        transpose_piece(2)
        quantize(2)

        rot_steps = [(j0 + jj, c) for j0, n in ORDER_GROUPS for c in range(4) for jj in range(n)]
        v_steps = [(j0, n, jj, c) for j0, n in V_GROUPS for c in (4, 5) for jj in range(n)]
        last_first, last_count = ORDER_GROUPS[-1]
        tail_start = len(rot_steps) - last_count

        def store_group(j, c):
            first, count = STORE_GROUPS[group_of(STORE_GROUPS, j)[0]]
            if first == last_first and c >= 3 - SPLIT_LAST:
                return j - j % PAIR, PAIR
            return first, count

        def add_and_store(engine, j, c, both, span):
            first, count = store_group(j, c)
            if j + 1 - span == first:
                rotated[c] = res.tile([P, HEADS, count, D], F32, name="rotated")
            add(engine, rotated[c], j + 1 - span - first, both, 0, span)
            if j + 1 == first + count:
                store(nc.sync, rotated[c], c, first, 0, count)

        v_done = 0
        both = v_res = None
        rotated = {}
        held = {}
        for s, (j, c) in enumerate(rot_steps):
            bank = rot_ps.tile([P, NCOL], F32, name="rot")
            project(bank, j, c)
            span = 1 if s < PAIR else PAIR if s < tail_start else last_count
            if (j - last_first) % span == 0:
                if s < tail_start:
                    both = prod.tile([P, HEADS, span, 2, D], F32, name="both")
                else:
                    both = keep.tile([P, HEADS, span, 2, D], F32, name="both_last")
            products(bank, j, both, (j - last_first) % span)
            if s in held:
                add_and_store(nc.vector, *held[s])
            if (j + 1) % span == 0 and s < tail_start:
                if s in VECTOR_ADDS_AT:
                    held[s + HOLD] = (j, c, both, span)
                else:
                    add_and_store(nc.gpsimd, j, c, both, span)

            if s in PREPARE_AFTER:
                xn = PREPARE_AFTER[s]
                transpose_piece(xn)
                quantize(xn)
                if xn == 3:
                    nc.scalar.copy(out=factors[1][:, :, 0:4:3, :], in_=cos_sb[1][:])
                    nc.scalar.copy(out=factors[1][:, :, 1, :], in_=sin_sb[1][:, :, 1, :])
                    nc.scalar.activation(
                        out=factors[1][:, :, 2, :], in_=sin_sb[1][:, :, 0, :], func=ACT.Copy, scale=-1.0
                    )

            v_due = min(len(v_steps), max(0, (s - V_FIRST + 1) * len(v_steps) // (V_LAST - V_FIRST + 1)))
            while v_done < v_due:
                vj0, vn, vjj, vc = v_steps[v_done]
                v_done += 1
                v_bank = aux_ps.tile([P, NCOL], F32, name="aux")
                project(v_bank, vj0 + vjj, vc)
                if vjj == 0:
                    v_res = v_pool.tile([P, HEADS, vn, D], F32, name="v_res")
                nc.scalar.copy(out=v_res[:, :, vjj, :], in_=v_bank[:].rearrange("p (h d) -> p h d", d=D))
                if vjj == vn - 1:
                    store(nc.scalar, v_res, vc, vj0, 0, vn)

        for h in range(0, HEADS, TAILH):
            last = res.tile([P, TAILH, last_count, D], F32, name="rotated")
            nc.vector.tensor_tensor(
                out=last[:], in0=both[:, h : h + TAILH, :, 0, :], in1=both[:, h : h + TAILH, :, 1, :], op=ALU.add
            )
            nc.sync.dma_start(
                out=outs[1][:, HEADS + h : HEADS + h + TAILH, last_first * D : TILES * D],
                in_=last[:].rearrange("p h j d -> p h (j d)"),
            )
